import numpy as np
import ml_dtypes


def mxq(x, axis, fmt="e4m3"):
    dtype, down = {"e4m3": (ml_dtypes.float8_e4m3fn, 7), "e5m2": (ml_dtypes.float8_e5m2, 14)}[fmt]
    v = np.moveaxis(np.asarray(x, np.float32).astype(ml_dtypes.bfloat16).astype(np.float64), axis, -1)
    blocks = v.reshape(v.shape[:-1] + (-1, 32))
    amax = np.abs(blocks).max(-1, keepdims=True)
    byte = np.maximum(np.where(amax > 0, np.frexp(amax)[1] - 1 + 127, 0) - down, 1)
    scale = np.exp2(byte - 127.0)
    codes = (blocks / scale).astype(np.float32).astype(dtype).astype(np.float64)
    return np.moveaxis((codes * scale).reshape(v.shape), -1, axis)


WIDE = False


def mx_kscale(k):
    if not WIDE:
        return np.ones(k)
    levels = np.array([10, -10, 5, -5, 0])
    if k % 512:
        return np.exp2(np.random.permutation(np.resize(levels, k // 32))).repeat(32)
    a = np.empty((k // 512, 16))
    for p in range(k // 512):
        a[p, :8] = np.random.permutation(np.resize(levels, 8))
        for g in range(8):
            far = levels[np.abs(levels - a[p, g]) >= 10]
            a[p, g + 8] = far[np.random.randint(len(far))]
    return np.exp2(a.ravel()).repeat(32)


BF16 = ml_dtypes.bfloat16


def bf(x):
    return np.asarray(x, np.float32).astype(BF16)


def f64(x):
    return np.asarray(x).astype(np.float64)


B, NC, APC, D = 512, 8, 512, 512
H = 2 * D
LN_EPS = 1e-5


def setup_inputs():
    s = mx_kscale(APC)
    t = np.exp2(np.round(np.log2(mx_kscale(H)) / 2))
    return {"tri": bf(np.random.standard_normal((B, APC * NC)) * np.repeat(s, NC)),
            "W1": bf(np.random.standard_normal((NC, APC, H)) / np.sqrt(APC) / s[None, :, None] * t),
            "b1": bf(np.random.standard_normal((NC, H)) * 0.1 * t),
            "W2": bf(np.random.standard_normal((NC, H, D)) / np.sqrt(H) / (t * t)[None, :, None]),
            "b2": bf(np.random.standard_normal((NC, D)) * 0.1),
            "gamma": bf(1.0 + 0.1 * np.random.standard_normal((NC, D))),
            "beta": bf(np.random.standard_normal((NC, D)) * 0.1)}


def reference(tri, W1, b1, W2, b2, gamma, beta):
    tri, W1, b1, W2, b2, gamma, beta = f64(tri), f64(W1), f64(b1), f64(W2), f64(b2), f64(gamma), f64(beta)
    b, n_anchors = tri.shape
    n_comp, apc, _ = W1.shape
    d = W2.shape[2]
    x = np.transpose(tri.reshape(b, apc, n_comp), (2, 0, 1))
    h = (mxq(x, 2, "e4m3") @ mxq(W1, 1, "e4m3")) + b1[:, None, :]
    h = np.square(np.maximum(h, 0.0))
    y = (mxq(h, 2, "e4m3") @ mxq(W2, 1, "e4m3")) + b2[:, None, :]
    mu = np.mean(y, axis=-1, keepdims=True)
    var = np.mean(np.square(y - mu), axis=-1, keepdims=True)
    y = (y - mu) * (1.0 / np.sqrt(var + LN_EPS))
    y = y * gamma[:, None, :] + beta[:, None, :]
    return np.transpose(y, (1, 0, 2)).reshape(b, n_comp * d)

@@ -1,0 +1,272 @@
+from contextlib import ExitStack
+
+import concourse.mybir as mybir
+from concourse.masks import make_identity
+
+F32 = mybir.dt.float32
+BF16 = mybir.dt.bfloat16
+U32 = mybir.dt.uint32
+U8 = mybir.dt.uint8
+FP8X4 = mybir.dt.float8_e4m3fn_x4
+ACT = mybir.ActivationFunctionType
+ALU = mybir.AluOpType
+
+B, NC, APC, D = 512, 8, 512, 512
+H = 2 * D
+LN_EPS = 1e-5
+P = 128
+NBT = B // P
+FLOPS = 2 * B * NC * (APC * H + H * D)
+
+BANK_DT = F32
+MANUAL = False
+FILL = [6,3,3,2,3,2,3,2]
+HEAD_STEPS = 9
+S_COPY = []
+
+
+def tile_patchwork_kernel(tc, tri, W1, b1, W2, b2, gamma, beta, out):
+    nc = tc.nc
+    with ExitStack() as ctx:
+        if MANUAL:
+            ctx.enter_context(tc.manual_schedule())
+        const = ctx.enter_context(tc.tile_pool(name="const", bufs=1))
+        raw = ctx.enter_context(tc.tile_pool(name="raw", bufs=4))
+        gw = ctx.enter_context(tc.tile_pool(name="gw", bufs=4))
+        wq = ctx.enter_context(tc.tile_pool(name="wq", bufs=8))
+        gx = ctx.enter_context(tc.tile_pool(name="gx", bufs=8))
+        hq = ctx.enter_context(tc.tile_pool(name="hq", bufs=4))
+        stats = ctx.enter_context(tc.tile_pool(name="stats", bufs=2))
+        psum = ctx.enter_context(tc.psum_pool(name="psum", bufs=8))
+
+        warm = const.tile([P, 1], F32, name="warm")
+        nc.vector.memset(warm[:], 0.0)
+        warm2 = const.tile([P, 1], F32, name="warm2")
+        nc.scalar.activation(out=warm2[:], in_=warm[:], func=ACT.Relu)
+        mhalf = const.tile([P, 2], F32, name="mhalf")
+        nc.vector.memset(mhalf[:], -0.5)
+        ident = const.tile([P, P], BF16, name="ident")
+        make_identity(nc, ident[:])
+        b1T = const.tile([P, 2 * NC, 4], BF16, name="b1T")
+        b2b = const.tile([P, NC * D], BF16, name="b2b")
+        gab = const.tile([P, NC * D], BF16, name="gab")
+        beb = const.tile([P, NC * D], BF16, name="beb")
+        xq = [const.tile([P, B], U32, name="xq%d" % k, align_bytes=64) for k in range(NC)]
+        xs = [const.tile([P, B], U8, name="xs%d" % k, align_bytes=64) for k in range(NC)]
+
+        raws = {}
+        gws = {}
+        wcodes = {}
+        state = {"step": 0, "qx": 0}
+
+        def load_w(c, s):
+            if s == 0:
+                t = raw.tile([P, 4, H], BF16, name="raw1", tag="raw")
+                nc.sync.dma_start(out=t[:], in_=W1[c].rearrange("(p j) h -> p j h", j=4))
+            else:
+                t = raw.tile([P, 2, 4, D], BF16, name="raw2", tag="raw")
+                nc.sync.dma_start(out=t[:], in_=W2[c].rearrange("(g p j) d -> p g j d", g=2, j=4))
+            raws[(c, s)] = t
+
+        def load_vectors():
+            nc.sync.dma_start(out=b2b[:], in_=b2.rearrange("k d -> (k d)").partition_broadcast(P))
+            nc.sync.dma_start(out=gab[:], in_=gamma.rearrange("k d -> (k d)").partition_broadcast(P))
+            nc.sync.dma_start(out=beb[:], in_=beta.rearrange("k d -> (k d)").partition_broadcast(P))
+
+        def copy_chunk(n):
+            c, s, g = n // 4, (n % 4) // 2, n % 2
+            t = gw.tile([P, 2048], BF16, name="gw", tag="gw", align_bytes=64)
+            if s == 0:
+                src = raws[(c, 0)][:, :, g * 512:(g + 1) * 512].rearrange("p j (m t) -> p t m j", t=4)
+                dst = t[:].rearrange("p (t m j) -> p t m j", t=4, j=4)
+            else:
+                src = raws[(c, 1)][:, g].rearrange("p j d -> p d j")
+                dst = t[:].rearrange("p (d j) -> p d j", j=4)
+            if n in S_COPY:
+                nc.scalar.copy(out=dst, in_=src)
+            else:
+                nc.vector.tensor_copy(out=dst, in_=src)
+            gws[n] = t
+            if g == 1 and c + 2 < NC:
+                load_w(c + 2, s)
+                if (c, s) == (1, 1):
+                    load_vectors()
+
+        def quant_chunk(n):
+            s = (n % 4) // 2
+            q = wq.tile([P, 512], U32, name="wcode", tag="w%dq" % s, align_bytes=64)
+            sc = wq.tile([P, 512], U8, name="wscale", tag="w%ds" % s, align_bytes=64)
+            nc.vector.quantize_mx(out=q[:].bitcast(FP8X4), scales=sc[:], in_=gws[n][:])
+            wcodes[n] = (q, sc)
+
+        def fill(count):
+            for rep in range(count):
+                n = state["step"]
+                if n < 4 * NC:
+                    copy_chunk(n)
+                if 1 <= n <= 4 * NC:
+                    quant_chunk(n - 1)
+                state["step"] = n + 1
+
+        gxs = {}
+
+        def xpose_evac(tri_sb, n):
+            bt, k = n // NC, n % NC
+            xt = psum.tile([P, 4, P], BF16, name="xt", tag="bank")
+            for t in range(4):
+                nc.tensor.transpose(xt[:, t, :], tri_sb[bt][:, 8 * t + k::32], ident[:])
+            g = gx.tile([P, 512], BF16, name="gx", tag="gx", align_bytes=64)
+            nc.scalar.copy(out=g[:].rearrange("p (b t) -> p b t", t=4), in_=xt[:].rearrange("p t b -> p b t"))
+            gxs[n] = g
+
+        def quant_x(upto):
+            while state["qx"] < min(upto, NBT * NC):
+                n = state["qx"]
+                bt, k = n // NC, n % NC
+                cols = slice(bt * P, (bt + 1) * P)
+                nc.vector.quantize_mx(out=xq[k][:, cols].bitcast(FP8X4), scales=xs[k][:, cols], in_=gxs[n][:])
+                state["qx"] = n + 1
+
+        banks = {}
+        rs = {}
+        ghs = {}
+        hcodes = {}
+
+        def mm1(k, g):
+            q, sc = wcodes[4 * k + g]
+            for t in range(4):
+                bank = psum.tile([P, B], BANK_DT, name="hbank", tag="bank")
+                cols = slice(t * P, (t + 1) * P)
+                nc.tensor.matmul_mx(out=bank[:], lhsT=q[:, cols].bitcast(FP8X4), lhsT_scale=sc[:, cols],
+                                    rhs=xq[k][:].bitcast(FP8X4), rhs_scale=xs[k][:], start=True, stop=True)
+                banks[(k, g, t)] = bank
+
+        def relu(late, k, g):
+            r = late["r"].tile([P, 4, B], F32, name="r", tag="r")
+            for t in range(4):
+                nc.scalar.activation(out=r[:, t, :], in_=banks[(k, g, t)][:], func=ACT.Relu,
+                                     bias=b1T[:, 2 * k + g, t:t + 1], scale=1.0)
+            rs[(k, g)] = r
+
+        def square(late, k, g):
+            t = late["gh"].tile([P, 4 * B], BF16, name="gh", tag="gh", align_bytes=64)
+            nc.scalar.activation(out=t[:].rearrange("p (b t) -> p b t", t=4),
+                                 in_=rs[(k, g)][:].rearrange("p t b -> p b t"), func=ACT.Square)
+            ghs[(k, g)] = t
+
+        def quant_h(k, g):
+            q = hq.tile([P, B], U32, name="hcode", tag="hq", align_bytes=64)
+            sc = hq.tile([P, B], U8, name="hscale", tag="hs", align_bytes=64)
+            nc.vector.quantize_mx(out=q[:].bitcast(FP8X4), scales=sc[:], in_=ghs[(k, g)][:])
+            hcodes[(k, g)] = (q, sc)
+
+        accs = {}
+        ys = {}
+        us = {}
+        st = {}
+
+        def mm2(k):
+            for bt in range(NBT):
+                acc = psum.tile([P, D], F32, name="acc", tag="bank")
+                cols = slice(bt * P, (bt + 1) * P)
+                for g in range(2):
+                    q, sc = hcodes[(k, g)]
+                    wc, ws = wcodes[4 * k + 2 + g]
+                    nc.tensor.matmul_mx(out=acc[:], lhsT=q[:, cols].bitcast(FP8X4), lhsT_scale=sc[:, cols],
+                                        rhs=wc[:].bitcast(FP8X4), rhs_scale=ws[:], start=(g == 0), stop=(g == 1))
+                accs[(k, bt)] = acc
+
+        def add_bias(late, k, pair):
+            if pair == 0:
+                st[k] = dict((nm, stats.tile([P, NBT], F32, name=nm, tag=nm))
+                             for nm in ("sums", "negmu", "ss", "var", "rstd"))
+            for bt in (2 * pair, 2 * pair + 1):
+                y = late["ln"].tile([P, D], F32, name="y", tag="y")
+                nc.vector.scalar_tensor_tensor(out=y[:], in0=accs[(k, bt)][:], scalar=1.0,
+                                               in1=b2b[:, k * D:(k + 1) * D], op0=ALU.mult, op1=ALU.add,
+                                               accum_out=st[k]["sums"][:, bt:bt + 1])
+                ys[(k, bt)] = y
+            cols = slice(2 * pair, 2 * pair + 2)
+            nc.gpsimd.tensor_scalar(out=st[k]["negmu"][:, cols], in0=st[k]["sums"][:, cols],
+                                    scalar1=-1.0 / D, scalar2=0.0, op0=ALU.mult, op1=ALU.add)
+
+        def variance(late, k, pair):
+            for bt in (2 * pair, 2 * pair + 1):
+                junk = late["ln"].tile([P, D], BF16, name="junk", tag="junk", bufs=2)
+                nc.scalar.activation(out=junk[:], in_=ys[(k, bt)][:], func=ACT.Square,
+                                     bias=st[k]["negmu"][:, bt:bt + 1], scale=1.0,
+                                     accum_out=st[k]["ss"][:, bt:bt + 1])
+            cols = slice(2 * pair, 2 * pair + 2)
+            nc.gpsimd.tensor_scalar(out=st[k]["var"][:, cols], in0=st[k]["ss"][:, cols],
+                                    scalar1=1.0 / D, scalar2=LN_EPS, op0=ALU.mult, op1=ALU.add)
+            nc.gpsimd.tensor_tensor(out=st[k]["rstd"][:, cols], in0=st[k]["var"][:, cols], in1=mhalf[:],
+                                    op=ALU.pow)
+
+        def centre_gain(late, k):
+            for bt in range(NBT):
+                u = late["ln"].tile([P, D], F32, name="u", tag="u")
+                nc.vector.scalar_tensor_tensor(out=u[:], in0=ys[(k, bt)][:], scalar=st[k]["negmu"][:, bt:bt + 1],
+                                               in1=gab[:, k * D:(k + 1) * D], op0=ALU.add, op1=ALU.mult)
+                us[(k, bt)] = u
+
+        def scale_shift_store(late, k, pair):
+            for bt in (2 * pair, 2 * pair + 1):
+                z = late["ln"].tile([P, D], F32, name="z", tag="z")
+                nc.vector.scalar_tensor_tensor(out=z[:], in0=us[(k, bt)][:], scalar=st[k]["rstd"][:, bt:bt + 1],
+                                               in1=beb[:, k * D:(k + 1) * D], op0=ALU.mult, op1=ALU.add)
+                nc.sync.dma_start(out=out[bt * P:(bt + 1) * P, k * D:(k + 1) * D], in_=z[:])
+
+        nc.sync.dma_start(out=b1T[:], in_=b1.rearrange("k (g p t) -> p (k g) t", g=2, t=4))
+        with tc.tile_pool(name="tri", bufs=1) as tri_pool:
+            tri_sb = [tri_pool.tile([P, NC * APC], BF16, name="tri%d" % bt) for bt in range(NBT)]
+            for i in range(NBT):
+                load_w(i // 2, i % 2)
+                nc.sync.dma_start(out=tri_sb[i][:], in_=tri[i * P:(i + 1) * P, :])
+            for j in range(HEAD_STEPS):
+                fill(1)
+                quant_x(4 * j - 3)
+                for n in range(4 * j, min(4 * j + 4, NBT * NC)):
+                    xpose_evac(tri_sb, n)
+
+        late = {"r": ctx.enter_context(tc.tile_pool(name="r", bufs=2)),
+                "gh": ctx.enter_context(tc.tile_pool(name="gh", bufs=2)),
+                "ln": ctx.enter_context(tc.tile_pool(name="ln", bufs=4))}
+        mm1(0, 0)
+
+        for i in range(NC + 1):
+            cur = i < NC
+            prev = i >= 1
+            share = [(FILL[i] + 3 - s) // 4 for s in range(4)] if cur else [0, 0, 0, 0]
+            if prev:
+                quant_h(i - 1, 1)
+                mm2(i - 1)
+            else:
+                quant_x(NBT * NC)
+            if cur:
+                relu(late, i, 0)
+                mm1(i, 1)
+            fill(share[0])
+            if prev:
+                add_bias(late, i - 1, 0)
+            if cur:
+                square(late, i, 0)
+            fill(share[1])
+            if prev:
+                add_bias(late, i - 1, 1)
+                variance(late, i - 1, 0)
+            if cur:
+                quant_h(i, 0)
+                if i + 1 < NC:
+                    mm1(i + 1, 0)
+                relu(late, i, 1)
+            if prev:
+                centre_gain(late, i - 1)
+                variance(late, i - 1, 1)
+            fill(share[2])
+            if prev:
+                scale_shift_store(late, i - 1, 0)
+            if cur:
+                square(late, i, 1)
+            fill(share[3])
+            if prev:
+                scale_shift_store(late, i - 1, 1)

@@ -20,9 +20,11 @@ FLOPS = 2 * B * NC * (APC * H + H * D)
 
 BANK_DT = F32
 MANUAL = False
+SIGMA = False
 FILL = [6,3,3,2,3,2,3,2]
-HEAD_STEPS = 9
 S_COPY = []
+HEAD_STEPS = 9
+NX = NBT * NC // 2
 
 
 def tile_patchwork_kernel(tc, tri, W1, b1, W2, b2, gamma, beta, out):
@@ -39,18 +41,22 @@ def tile_patchwork_kernel(tc, tri, W1, b1, W2, b2, gamma, beta, out):
         stats = ctx.enter_context(tc.tile_pool(name="stats", bufs=2))
         psum = ctx.enter_context(tc.psum_pool(name="psum", bufs=8))
 
+        eps = const.tile([P, 1], F32, name="eps")
+        nc.vector.memset(eps[:], LN_EPS)
         warm = const.tile([P, 1], F32, name="warm")
-        nc.vector.memset(warm[:], 0.0)
-        warm2 = const.tile([P, 1], F32, name="warm2")
-        nc.scalar.activation(out=warm2[:], in_=warm[:], func=ACT.Relu)
-        mhalf = const.tile([P, 2], F32, name="mhalf")
-        nc.vector.memset(mhalf[:], -0.5)
+        nc.scalar.activation(out=warm[:], in_=eps[:], func=ACT.Sqrt)
+        vrows = [const.tile([P, D], BF16, name="vrows%d" % v) for v in range(3)]
+        for v in range(3):
+            nc.vector.memset(vrows[v][:], 0.0)
         ident = const.tile([P, P], BF16, name="ident")
         make_identity(nc, ident[:])
-        b1T = const.tile([P, 2 * NC, 4], BF16, name="b1T")
+        identw = const.tile([P, P], F32, name="identw")
+        make_identity(nc, identw[:])
+        b1rows = const.tile([P, 512], BF16, name="b1rows")
+        nc.vector.memset(b1rows[:], 0.0)
+        b1cols = const.tile([P, 4, P], BF16, name="b1cols")
+        b1T = const.tile([P, 4, 2 * NC], BF16, name="b1T")
         b2b = const.tile([P, NC * D], BF16, name="b2b")
-        gab = const.tile([P, NC * D], BF16, name="gab")
-        beb = const.tile([P, NC * D], BF16, name="beb")
         xq = [const.tile([P, B], U32, name="xq%d" % k, align_bytes=64) for k in range(NC)]
         xs = [const.tile([P, B], U8, name="xs%d" % k, align_bytes=64) for k in range(NC)]
 
@@ -63,34 +69,40 @@ def tile_patchwork_kernel(tc, tri, W1, b1, W2, b2, gamma, beta, out):
             if s == 0:
                 t = raw.tile([P, 4, H], BF16, name="raw1", tag="raw")
                 nc.sync.dma_start(out=t[:], in_=W1[c].rearrange("(p j) h -> p j h", j=4))
-            else:
+            elif not SIGMA:
                 t = raw.tile([P, 2, 4, D], BF16, name="raw2", tag="raw")
                 nc.sync.dma_start(out=t[:], in_=W2[c].rearrange("(g p j) d -> p g j d", g=2, j=4))
+            else:
+                t = raw.tile([P, 2, 4, D], BF16, name="raw2", tag="raw")
+                rows = W2[c].rearrange("(g q j r) d -> g j q r d", g=2, j=4, r=8)
+                for g in range(2):
+                    for j in range(4):
+                        nc.sync.dma_start(out=t[:, g, j, :], in_=rows[g, j].rearrange("q r d -> (q r) d"))
             raws[(c, s)] = t
 
-        def load_vectors():
-            nc.sync.dma_start(out=b2b[:], in_=b2.rearrange("k d -> (k d)").partition_broadcast(P))
-            nc.sync.dma_start(out=gab[:], in_=gamma.rearrange("k d -> (k d)").partition_broadcast(P))
-            nc.sync.dma_start(out=beb[:], in_=beta.rearrange("k d -> (k d)").partition_broadcast(P))
+        def spread(dst, v, row):
+            nc.tensor.matmul(out=dst, lhsT=ident[:, row:row + 1].to_broadcast([P, P]), rhs=vrows[v][:], start=True, stop=True)
 
         def copy_chunk(n):
             c, s, g = n // 4, (n % 4) // 2, n % 2
             t = gw.tile([P, 2048], BF16, name="gw", tag="gw", align_bytes=64)
-            if s == 0:
+            if s == 0 and not SIGMA:
                 src = raws[(c, 0)][:, :, g * 512:(g + 1) * 512].rearrange("p j (m t) -> p t m j", t=4)
-                dst = t[:].rearrange("p (t m j) -> p t m j", t=4, j=4)
+                nc.vector.tensor_copy(out=t[:].rearrange("p (t m j) -> p t m j", t=4, j=4), in_=src)
+            elif s == 0:
+                src = raws[(c, 0)][:, :, g * 512:(g + 1) * 512].rearrange("p j (q t r) -> p t q r j", t=4, r=8)
+                dst = t[:].rearrange("p (t q r j) -> p t q r j", t=4, r=8, j=4)
+                for tt in range(4):
+                    nc.vector.tensor_copy(out=dst[:, tt], in_=src[:, tt])
+            elif n in S_COPY:
+                nc.scalar.copy(out=t[:].rearrange("p (d j) -> p d j", j=4),
+                               in_=raws[(c, 1)][:, g].rearrange("p j d -> p d j"))
             else:
-                src = raws[(c, 1)][:, g].rearrange("p j d -> p d j")
-                dst = t[:].rearrange("p (d j) -> p d j", j=4)
-            if n in S_COPY:
-                nc.scalar.copy(out=dst, in_=src)
-            else:
-                nc.vector.tensor_copy(out=dst, in_=src)
+                nc.vector.tensor_copy(out=t[:].rearrange("p (d j) -> p d j", j=4),
+                                      in_=raws[(c, 1)][:, g].rearrange("p j d -> p d j"))
             gws[n] = t
             if g == 1 and c + 2 < NC:
                 load_w(c + 2, s)
-                if (c, s) == (1, 1):
-                    load_vectors()
 
         def quant_chunk(n):
             s = (n % 4) // 2
@@ -111,16 +123,19 @@ def tile_patchwork_kernel(tc, tri, W1, b1, W2, b2, gamma, beta, out):
         gxs = {}
 
         def xpose_evac(tri_sb, n):
-            bt, k = n // NC, n % NC
-            xt = psum.tile([P, 4, P], BF16, name="xt", tag="bank")
+            bt, pair = n // (NC // 2), n % (NC // 2)
+            words = tri_sb[bt][:].bitcast(F32)
+            xt = psum.tile([P, 4, P], F32, name="xt", tag="bank")
             for t in range(4):
-                nc.tensor.transpose(xt[:, t, :], tri_sb[bt][:, 8 * t + k::32], ident[:])
-            g = gx.tile([P, 512], BF16, name="gx", tag="gx", align_bytes=64)
-            nc.scalar.copy(out=g[:].rearrange("p (b t) -> p b t", t=4), in_=xt[:].rearrange("p t b -> p b t"))
-            gxs[n] = g
+                nc.tensor.transpose(xt[:, t, :], words[:, 4 * t + pair::16], identw[:])
+            halves = xt[:].rearrange("p t b -> p (t b)").bitcast(BF16).rearrange("p (t b e) -> p e b t", t=4, e=2)
+            for e in range(2):
+                g = gx.tile([P, 512], BF16, name="gx", tag="gx", align_bytes=64)
+                nc.scalar.copy(out=g[:].rearrange("p (b t) -> p b t", t=4), in_=halves[:, e])
+                gxs[2 * n + e] = g
 
         def quant_x(upto):
-            while state["qx"] < min(upto, NBT * NC):
+            while state["qx"] < min(upto, 2 * NX):
                 n = state["qx"]
                 bt, k = n // NC, n % NC
                 cols = slice(bt * P, (bt + 1) * P)
@@ -145,7 +160,7 @@ def tile_patchwork_kernel(tc, tri, W1, b1, W2, b2, gamma, beta, out):
             r = late["r"].tile([P, 4, B], F32, name="r", tag="r")
             for t in range(4):
                 nc.scalar.activation(out=r[:, t, :], in_=banks[(k, g, t)][:], func=ACT.Relu,
-                                     bias=b1T[:, 2 * k + g, t:t + 1], scale=1.0)
+                                     bias=b1T[:, t, 2 * k + g:2 * k + g + 1], scale=1.0)
             rs[(k, g)] = r
 
         def square(late, k, g):
@@ -164,6 +179,7 @@ def tile_patchwork_kernel(tc, tri, W1, b1, W2, b2, gamma, beta, out):
         ys = {}
         us = {}
         st = {}
+        gbs = {}
 
         def mm2(k):
             for bt in range(NBT):
@@ -175,57 +191,81 @@ def tile_patchwork_kernel(tc, tri, W1, b1, W2, b2, gamma, beta, out):
                     nc.tensor.matmul_mx(out=acc[:], lhsT=q[:, cols].bitcast(FP8X4), lhsT_scale=sc[:, cols],
                                         rhs=wc[:].bitcast(FP8X4), rhs_scale=ws[:], start=(g == 0), stop=(g == 1))
                 accs[(k, bt)] = acc
+            gb = psum.tile([P, 2, D], BF16, name="gb", tag="bank")
+            spread(gb[:, 0, :], 1, k)
+            spread(gb[:, 1, :], 2, k)
+            gbs[k] = gb
 
-        def add_bias(late, k, pair):
-            if pair == 0:
+        def add_bias(late, k, bts):
+            if bts[0] == 0:
                 st[k] = dict((nm, stats.tile([P, NBT], F32, name=nm, tag=nm))
-                             for nm in ("sums", "negmu", "ss", "var", "rstd"))
-            for bt in (2 * pair, 2 * pair + 1):
+                             for nm in ("sums", "negmu", "ss", "std", "rstd"))
+            for bt in bts:
                 y = late["ln"].tile([P, D], F32, name="y", tag="y")
                 nc.vector.scalar_tensor_tensor(out=y[:], in0=accs[(k, bt)][:], scalar=1.0,
                                                in1=b2b[:, k * D:(k + 1) * D], op0=ALU.mult, op1=ALU.add,
                                                accum_out=st[k]["sums"][:, bt:bt + 1])
                 ys[(k, bt)] = y
+
+        def mean(k, pair):
             cols = slice(2 * pair, 2 * pair + 2)
-            nc.gpsimd.tensor_scalar(out=st[k]["negmu"][:, cols], in0=st[k]["sums"][:, cols],
-                                    scalar1=-1.0 / D, scalar2=0.0, op0=ALU.mult, op1=ALU.add)
+            nc.vector.tensor_scalar(out=st[k]["negmu"][:, cols], in0=st[k]["sums"][:, cols], scalar1=-1.0 / D, scalar2=0.0,
+                                    op0=ALU.mult, op1=ALU.add)
 
         def variance(late, k, pair):
+            cols = slice(2 * pair, 2 * pair + 2)
             for bt in (2 * pair, 2 * pair + 1):
                 junk = late["ln"].tile([P, D], BF16, name="junk", tag="junk", bufs=2)
                 nc.scalar.activation(out=junk[:], in_=ys[(k, bt)][:], func=ACT.Square,
                                      bias=st[k]["negmu"][:, bt:bt + 1], scale=1.0,
                                      accum_out=st[k]["ss"][:, bt:bt + 1])
-            cols = slice(2 * pair, 2 * pair + 2)
-            nc.gpsimd.tensor_scalar(out=st[k]["var"][:, cols], in0=st[k]["ss"][:, cols],
-                                    scalar1=1.0 / D, scalar2=LN_EPS, op0=ALU.mult, op1=ALU.add)
-            nc.gpsimd.tensor_tensor(out=st[k]["rstd"][:, cols], in0=st[k]["var"][:, cols], in1=mhalf[:],
-                                    op=ALU.pow)
+            nc.scalar.activation(out=st[k]["std"][:, cols], in_=st[k]["ss"][:, cols], func=ACT.Sqrt,
+                                 bias=eps[:], scale=1.0 / D)
 
-        def centre_gain(late, k):
-            for bt in range(NBT):
+        def centre_gain(late, k, pair):
+            for bt in (2 * pair, 2 * pair + 1):
                 u = late["ln"].tile([P, D], F32, name="u", tag="u")
                 nc.vector.scalar_tensor_tensor(out=u[:], in0=ys[(k, bt)][:], scalar=st[k]["negmu"][:, bt:bt + 1],
-                                               in1=gab[:, k * D:(k + 1) * D], op0=ALU.add, op1=ALU.mult)
+                                               in1=gbs[k][:, 0, :], op0=ALU.add, op1=ALU.mult)
                 us[(k, bt)] = u
+
+        def invert(k, pair):
+            cols = slice(2 * pair, 2 * pair + 2)
+            nc.vector.reciprocal(out=st[k]["rstd"][:, cols], in_=st[k]["std"][:, cols])
 
         def scale_shift_store(late, k, pair):
             for bt in (2 * pair, 2 * pair + 1):
                 z = late["ln"].tile([P, D], F32, name="z", tag="z")
                 nc.vector.scalar_tensor_tensor(out=z[:], in0=us[(k, bt)][:], scalar=st[k]["rstd"][:, bt:bt + 1],
-                                               in1=beb[:, k * D:(k + 1) * D], op0=ALU.mult, op1=ALU.add)
+                                               in1=gbs[k][:, 1, :], op0=ALU.mult, op1=ALU.add)
                 nc.sync.dma_start(out=out[bt * P:(bt + 1) * P, k * D:(k + 1) * D], in_=z[:])
 
-        nc.sync.dma_start(out=b1T[:], in_=b1.rearrange("k (g p t) -> p (k g) t", g=2, t=4))
         with tc.tile_pool(name="tri", bufs=1) as tri_pool:
             tri_sb = [tri_pool.tile([P, NC * APC], BF16, name="tri%d" % bt) for bt in range(NBT)]
+            nc.sync.dma_start(out=b1rows[0:2 * NC, :], in_=b1.rearrange("k (g c) -> (k g) c", g=2))
+            for v, vec in enumerate((b2, gamma, beta)):
+                nc.sync.dma_start(out=vrows[v][0:NC, :], in_=vec)
             for i in range(NBT):
                 load_w(i // 2, i % 2)
                 nc.sync.dma_start(out=tri_sb[i][:], in_=tri[i * P:(i + 1) * P, :])
+            if SIGMA:
+                nc.vector.tensor_copy(out=b1cols[:].rearrange("p t (q r) -> p t q r", r=8),
+                                      in_=b1rows[:].rearrange("p (q t r) -> p t q r", t=4, r=8))
+            else:
+                nc.vector.tensor_copy(out=b1cols[:], in_=b1rows[:].rearrange("p (m t) -> p t m", t=4))
+            b1p = psum.tile([P, 4, P], BF16, name="b1p", tag="bank")
+            for t in range(4):
+                nc.tensor.transpose(b1p[:, t, :], b1cols[:, t, :], ident[:])
+            nc.scalar.copy(out=b1T[:], in_=b1p[:, :, 0:2 * NC])
+            for kk in range(NC // 2):
+                bb = psum.tile([P, 2, D], BF16, name="bb", tag="bank")
+                spread(bb[:, 0, :], 0, 2 * kk)
+                spread(bb[:, 1, :], 0, 2 * kk + 1)
+                nc.scalar.copy(out=b2b[:, 2 * kk * D:(2 * kk + 2) * D], in_=bb[:].rearrange("p a d -> p (a d)"))
             for j in range(HEAD_STEPS):
                 fill(1)
                 quant_x(4 * j - 3)
-                for n in range(4 * j, min(4 * j + 4, NBT * NC)):
+                for n in range(2 * j, min(2 * j + 2, NX)):
                     xpose_evac(tri_sb, n)
 
         late = {"r": ctx.enter_context(tc.tile_pool(name="r", bufs=2)),
@@ -241,18 +281,20 @@ def tile_patchwork_kernel(tc, tri, W1, b1, W2, b2, gamma, beta, out):
                 quant_h(i - 1, 1)
                 mm2(i - 1)
             else:
-                quant_x(NBT * NC)
+                quant_x(2 * NX)
             if cur:
                 relu(late, i, 0)
                 mm1(i, 1)
             fill(share[0])
             if prev:
-                add_bias(late, i - 1, 0)
+                add_bias(late, i - 1, (0, 1, 2))
+                mean(i - 1, 0)
+                add_bias(late, i - 1, (3,))
             if cur:
                 square(late, i, 0)
             fill(share[1])
             if prev:
-                add_bias(late, i - 1, 1)
+                mean(i - 1, 1)
                 variance(late, i - 1, 0)
             if cur:
                 quant_h(i, 0)
@@ -260,10 +302,13 @@ def tile_patchwork_kernel(tc, tri, W1, b1, W2, b2, gamma, beta, out):
                     mm1(i + 1, 0)
                 relu(late, i, 1)
             if prev:
-                centre_gain(late, i - 1)
+                invert(i - 1, 0)
+                centre_gain(late, i - 1, 0)
+                centre_gain(late, i - 1, 1)
                 variance(late, i - 1, 1)
             fill(share[2])
             if prev:
+                invert(i - 1, 1)
                 scale_shift_store(late, i - 1, 0)
             if cur:
                 square(late, i, 1)

@@ -22,6 +22,7 @@ BANK_DT = F32
 MANUAL = False
 SIGMA = False
 FILL = [6,3,3,2,3,2,3,2]
+PE_CHUNKS = []
 S_COPY = []
 HEAD_STEPS = 9
 NX = NBT * NC // 2
@@ -86,9 +87,21 @@ def tile_patchwork_kernel(tc, tri, W1, b1, W2, b2, gamma, beta, out):
         def copy_chunk(n):
             c, s, g = n // 4, (n % 4) // 2, n % 2
             t = gw.tile([P, 2048], BF16, name="gw", tag="gw", align_bytes=64)
-            if s == 0 and not SIGMA:
-                src = raws[(c, 0)][:, :, g * 512:(g + 1) * 512].rearrange("p j (m t) -> p t m j", t=4)
-                nc.vector.tensor_copy(out=t[:].rearrange("p (t m j) -> p t m j", t=4, j=4), in_=src)
+            if n in PE_CHUNKS:
+                for half in range(2):
+                    wb = psum.tile([P, 1024], BF16, name="wbank", tag="bank")
+                    for q in range(2):
+                        piece = 2 * half + q
+                        if s == 0:
+                            mov = raws[(c, 0)][:, :, g * 512 + piece:(g + 1) * 512:4].rearrange("p j m -> p m j")
+                        else:
+                            mov = raws[(c, 1)][:, g, :, piece * P:(piece + 1) * P].rearrange("p j d -> p d j")
+                        nc.tensor.matmul(out=wb[:, q * 512:(q + 1) * 512].rearrange("p (m j) -> p m j", j=4),
+                                         lhsT=ident[:], rhs=mov, start=True, stop=True)
+                    nc.scalar.copy(out=t[:, half * 1024:(half + 1) * 1024], in_=wb[:])
+            elif s == 0 and not SIGMA:
+                src = raws[(c, 0)][:, :, g * 512:(g + 1) * 512].rearrange("p j (m t) -> p m j t", t=4)
+                nc.vector.tensor_copy(out=t[:].rearrange("p (t m j) -> p m j t", t=4, j=4), in_=src)
             elif s == 0:
                 src = raws[(c, 0)][:, :, g * 512:(g + 1) * 512].rearrange("p j (q t r) -> p t q r j", t=4, r=8)
                 dst = t[:].rearrange("p (t q r j) -> p t q r j", t=4, r=8, j=4)
@@ -98,8 +111,8 @@ def tile_patchwork_kernel(tc, tri, W1, b1, W2, b2, gamma, beta, out):
                 nc.scalar.copy(out=t[:].rearrange("p (d j) -> p d j", j=4),
                                in_=raws[(c, 1)][:, g].rearrange("p j d -> p d j"))
             else:
-                nc.vector.tensor_copy(out=t[:].rearrange("p (d j) -> p d j", j=4),
-                                      in_=raws[(c, 1)][:, g].rearrange("p j d -> p d j"))
+                nc.vector.tensor_copy(out=t[:].rearrange("p (c i j) -> p c j i", i=4, j=4),
+                                      in_=raws[(c, 1)][:, g].rearrange("p j (c i) -> p c j i", i=4))
             gws[n] = t
             if g == 1 and c + 2 < NC:
                 load_w(c + 2, s)
@@ -165,8 +178,8 @@ def tile_patchwork_kernel(tc, tri, W1, b1, W2, b2, gamma, beta, out):
 
         def square(late, k, g):
             t = late["gh"].tile([P, 4 * B], BF16, name="gh", tag="gh", align_bytes=64)
-            nc.scalar.activation(out=t[:].rearrange("p (b t) -> p b t", t=4),
-                                 in_=rs[(k, g)][:].rearrange("p t b -> p b t"), func=ACT.Square)
+            nc.scalar.activation(out=t[:].rearrange("p (c i t) -> p c t i", i=4, t=4),
+                                 in_=rs[(k, g)][:].rearrange("p t (c i) -> p c t i", i=4), func=ACT.Square)
             ghs[(k, g)] = t
 
         def quant_h(k, g):

from contextlib import ExitStack

import concourse.mybir as mybir
from concourse.masks import make_identity

F32 = mybir.dt.float32
BF16 = mybir.dt.bfloat16
U32 = mybir.dt.uint32
U8 = mybir.dt.uint8
FP8X4 = mybir.dt.float8_e4m3fn_x4
ACT = mybir.ActivationFunctionType
ALU = mybir.AluOpType

B, NC, APC, D = 512, 8, 512, 512
H = 2 * D
LN_EPS = 1e-5
P = 128
NBT = B // P
FLOPS = 2 * B * NC * (APC * H + H * D)

BANK_DT = F32
MANUAL = False
SIGMA = False
FILL = [6,3,3,2,3,2,3,2]
PE_CHUNKS = []
S_COPY = []
HEAD_STEPS = 9
NX = NBT * NC // 2


def tile_patchwork_kernel(tc, tri, W1, b1, W2, b2, gamma, beta, out):
    nc = tc.nc
    with ExitStack() as ctx:
        if MANUAL:
            ctx.enter_context(tc.manual_schedule())
        const = ctx.enter_context(tc.tile_pool(name="const", bufs=1))
        raw = ctx.enter_context(tc.tile_pool(name="raw", bufs=4))
        gw = ctx.enter_context(tc.tile_pool(name="gw", bufs=4))
        wq = ctx.enter_context(tc.tile_pool(name="wq", bufs=8))
        gx = ctx.enter_context(tc.tile_pool(name="gx", bufs=8))
        hq = ctx.enter_context(tc.tile_pool(name="hq", bufs=4))
        stats = ctx.enter_context(tc.tile_pool(name="stats", bufs=2))
        psum = ctx.enter_context(tc.psum_pool(name="psum", bufs=8))

        eps = const.tile([P, 1], F32, name="eps")
        nc.vector.memset(eps[:], LN_EPS)
        warm = const.tile([P, 1], F32, name="warm")
        nc.scalar.activation(out=warm[:], in_=eps[:], func=ACT.Sqrt)
        vrows = [const.tile([P, D], BF16, name="vrows%d" % v) for v in range(3)]
        for v in range(3):
            nc.vector.memset(vrows[v][:], 0.0)
        ident = const.tile([P, P], BF16, name="ident")
        make_identity(nc, ident[:])
        identw = const.tile([P, P], F32, name="identw")
        make_identity(nc, identw[:])
        b1rows = const.tile([P, 512], BF16, name="b1rows")
        nc.vector.memset(b1rows[:], 0.0)
        b1cols = const.tile([P, 4, P], BF16, name="b1cols")
        b1T = const.tile([P, 4, 2 * NC], BF16, name="b1T")
        b2b = const.tile([P, NC * D], BF16, name="b2b")
        xq = [const.tile([P, B], U32, name="xq%d" % k, align_bytes=64) for k in range(NC)]
        xs = [const.tile([P, B], U8, name="xs%d" % k, align_bytes=64) for k in range(NC)]

        raws = {}
        gws = {}
        wcodes = {}
        state = {"step": 0, "qx": 0}

        def load_w(c, s):
            if s == 0:
                t = raw.tile([P, 4, H], BF16, name="raw1", tag="raw")
                nc.sync.dma_start(out=t[:], in_=W1[c].rearrange("(p j) h -> p j h", j=4))
            elif not SIGMA:
                t = raw.tile([P, 2, 4, D], BF16, name="raw2", tag="raw")
                nc.sync.dma_start(out=t[:], in_=W2[c].rearrange("(g p j) d -> p g j d", g=2, j=4))
            else:
                t = raw.tile([P, 2, 4, D], BF16, name="raw2", tag="raw")
                rows = W2[c].rearrange("(g q j r) d -> g j q r d", g=2, j=4, r=8)
                for g in range(2):
                    for j in range(4):
                        nc.sync.dma_start(out=t[:, g, j, :], in_=rows[g, j].rearrange("q r d -> (q r) d"))
            raws[(c, s)] = t

        def spread(dst, v, row):
            nc.tensor.matmul(out=dst, lhsT=ident[:, row:row + 1].to_broadcast([P, P]), rhs=vrows[v][:], start=True, stop=True)

        def copy_chunk(n):
            c, s, g = n // 4, (n % 4) // 2, n % 2
            t = gw.tile([P, 2048], BF16, name="gw", tag="gw", align_bytes=64)
            if n in PE_CHUNKS:
                for half in range(2):
                    wb = psum.tile([P, 1024], BF16, name="wbank", tag="bank")
                    for q in range(2):
                        piece = 2 * half + q
                        if s == 0:
                            mov = raws[(c, 0)][:, :, g * 512 + piece:(g + 1) * 512:4].rearrange("p j m -> p m j")
                        else:
                            mov = raws[(c, 1)][:, g, :, piece * P:(piece + 1) * P].rearrange("p j d -> p d j")
                        nc.tensor.matmul(out=wb[:, q * 512:(q + 1) * 512].rearrange("p (m j) -> p m j", j=4),
                                         lhsT=ident[:], rhs=mov, start=True, stop=True)
                    nc.scalar.copy(out=t[:, half * 1024:(half + 1) * 1024], in_=wb[:])
            elif s == 0 and not SIGMA:
                src = raws[(c, 0)][:, :, g * 512:(g + 1) * 512].rearrange("p j (m t) -> p m j t", t=4)
                nc.vector.tensor_copy(out=t[:].rearrange("p (t m j) -> p m j t", t=4, j=4), in_=src)
            elif s == 0:
                src = raws[(c, 0)][:, :, g * 512:(g + 1) * 512].rearrange("p j (q t r) -> p t q r j", t=4, r=8)
                dst = t[:].rearrange("p (t q r j) -> p t q r j", t=4, r=8, j=4)
                for tt in range(4):
                    nc.vector.tensor_copy(out=dst[:, tt], in_=src[:, tt])
            elif n in S_COPY:
                nc.scalar.copy(out=t[:].rearrange("p (d j) -> p d j", j=4),
                               in_=raws[(c, 1)][:, g].rearrange("p j d -> p d j"))
            else:
                nc.vector.tensor_copy(out=t[:].rearrange("p (c i j) -> p c j i", i=4, j=4),
                                      in_=raws[(c, 1)][:, g].rearrange("p j (c i) -> p c j i", i=4))
            gws[n] = t
            if g == 1 and c + 2 < NC:
                load_w(c + 2, s)

        def quant_chunk(n):
            s = (n % 4) // 2
            q = wq.tile([P, 512], U32, name="wcode", tag="w%dq" % s, align_bytes=64)
            sc = wq.tile([P, 512], U8, name="wscale", tag="w%ds" % s, align_bytes=64)
            nc.vector.quantize_mx(out=q[:].bitcast(FP8X4), scales=sc[:], in_=gws[n][:])
            wcodes[n] = (q, sc)

        def fill(count):
            for rep in range(count):
                n = state["step"]
                if n < 4 * NC:
                    copy_chunk(n)
                if 1 <= n <= 4 * NC:
                    quant_chunk(n - 1)
                state["step"] = n + 1

        gxs = {}

        def xpose_evac(tri_sb, n):
            bt, pair = n // (NC // 2), n % (NC // 2)
            words = tri_sb[bt][:].bitcast(F32)
            xt = psum.tile([P, 4, P], F32, name="xt", tag="bank")
            for t in range(4):
                nc.tensor.transpose(xt[:, t, :], words[:, 4 * t + pair::16], identw[:])
            halves = xt[:].rearrange("p t b -> p (t b)").bitcast(BF16).rearrange("p (t b e) -> p e b t", t=4, e=2)
            for e in range(2):
                g = gx.tile([P, 512], BF16, name="gx", tag="gx", align_bytes=64)
                nc.scalar.copy(out=g[:].rearrange("p (b t) -> p b t", t=4), in_=halves[:, e])
                gxs[2 * n + e] = g

        def quant_x(upto):
            while state["qx"] < min(upto, 2 * NX):
                n = state["qx"]
                bt, k = n // NC, n % NC
                cols = slice(bt * P, (bt + 1) * P)
                nc.vector.quantize_mx(out=xq[k][:, cols].bitcast(FP8X4), scales=xs[k][:, cols], in_=gxs[n][:])
                state["qx"] = n + 1

        banks = {}
        rs = {}
        ghs = {}
        hcodes = {}

        def mm1(k, g):
            q, sc = wcodes[4 * k + g]
            for t in range(4):
                bank = psum.tile([P, B], BANK_DT, name="hbank", tag="bank")
                cols = slice(t * P, (t + 1) * P)
                nc.tensor.matmul_mx(out=bank[:], lhsT=q[:, cols].bitcast(FP8X4), lhsT_scale=sc[:, cols],
                                    rhs=xq[k][:].bitcast(FP8X4), rhs_scale=xs[k][:], start=True, stop=True)
                banks[(k, g, t)] = bank

        def relu(late, k, g):
            r = late["r"].tile([P, 4, B], F32, name="r", tag="r")
            for t in range(4):
                nc.scalar.activation(out=r[:, t, :], in_=banks[(k, g, t)][:], func=ACT.Relu,
                                     bias=b1T[:, t, 2 * k + g:2 * k + g + 1], scale=1.0)
            rs[(k, g)] = r

        def square(late, k, g):
            t = late["gh"].tile([P, 4 * B], BF16, name="gh", tag="gh", align_bytes=64)
            nc.scalar.activation(out=t[:].rearrange("p (c i t) -> p c t i", i=4, t=4),
                                 in_=rs[(k, g)][:].rearrange("p t (c i) -> p c t i", i=4), func=ACT.Square)
            ghs[(k, g)] = t

        def quant_h(k, g):
            q = hq.tile([P, B], U32, name="hcode", tag="hq", align_bytes=64)
            sc = hq.tile([P, B], U8, name="hscale", tag="hs", align_bytes=64)
            nc.vector.quantize_mx(out=q[:].bitcast(FP8X4), scales=sc[:], in_=ghs[(k, g)][:])
            hcodes[(k, g)] = (q, sc)

        accs = {}
        ys = {}
        us = {}
        st = {}
        gbs = {}

        def mm2(k):
            for bt in range(NBT):
                acc = psum.tile([P, D], F32, name="acc", tag="bank")
                cols = slice(bt * P, (bt + 1) * P)
                for g in range(2):
                    q, sc = hcodes[(k, g)]
                    wc, ws = wcodes[4 * k + 2 + g]
                    nc.tensor.matmul_mx(out=acc[:], lhsT=q[:, cols].bitcast(FP8X4), lhsT_scale=sc[:, cols],
                                        rhs=wc[:].bitcast(FP8X4), rhs_scale=ws[:], start=(g == 0), stop=(g == 1))
                accs[(k, bt)] = acc
            gb = psum.tile([P, 2, D], BF16, name="gb", tag="bank")
            spread(gb[:, 0, :], 1, k)
            spread(gb[:, 1, :], 2, k)
            gbs[k] = gb

        def add_bias(late, k, bts):
            if bts[0] == 0:
                st[k] = dict((nm, stats.tile([P, NBT], F32, name=nm, tag=nm))
                             for nm in ("sums", "negmu", "ss", "std", "rstd"))
            for bt in bts:
                y = late["ln"].tile([P, D], F32, name="y", tag="y")
                nc.vector.scalar_tensor_tensor(out=y[:], in0=accs[(k, bt)][:], scalar=1.0,
                                               in1=b2b[:, k * D:(k + 1) * D], op0=ALU.mult, op1=ALU.add,
                                               accum_out=st[k]["sums"][:, bt:bt + 1])
                ys[(k, bt)] = y

        def mean(k, pair):
            cols = slice(2 * pair, 2 * pair + 2)
            nc.vector.tensor_scalar(out=st[k]["negmu"][:, cols], in0=st[k]["sums"][:, cols], scalar1=-1.0 / D, scalar2=0.0,
                                    op0=ALU.mult, op1=ALU.add)

        def variance(late, k, pair):
            cols = slice(2 * pair, 2 * pair + 2)
            for bt in (2 * pair, 2 * pair + 1):
                junk = late["ln"].tile([P, D], BF16, name="junk", tag="junk", bufs=2)
                nc.scalar.activation(out=junk[:], in_=ys[(k, bt)][:], func=ACT.Square,
                                     bias=st[k]["negmu"][:, bt:bt + 1], scale=1.0,
                                     accum_out=st[k]["ss"][:, bt:bt + 1])
            nc.scalar.activation(out=st[k]["std"][:, cols], in_=st[k]["ss"][:, cols], func=ACT.Sqrt,
                                 bias=eps[:], scale=1.0 / D)

        def centre_gain(late, k, pair):
            for bt in (2 * pair, 2 * pair + 1):
                u = late["ln"].tile([P, D], F32, name="u", tag="u")
                nc.vector.scalar_tensor_tensor(out=u[:], in0=ys[(k, bt)][:], scalar=st[k]["negmu"][:, bt:bt + 1],
                                               in1=gbs[k][:, 0, :], op0=ALU.add, op1=ALU.mult)
                us[(k, bt)] = u

        def invert(k, pair):
            cols = slice(2 * pair, 2 * pair + 2)
            nc.vector.reciprocal(out=st[k]["rstd"][:, cols], in_=st[k]["std"][:, cols])

        def scale_shift_store(late, k, pair):
            for bt in (2 * pair, 2 * pair + 1):
                z = late["ln"].tile([P, D], F32, name="z", tag="z")
                nc.vector.scalar_tensor_tensor(out=z[:], in0=us[(k, bt)][:], scalar=st[k]["rstd"][:, bt:bt + 1],
                                               in1=gbs[k][:, 1, :], op0=ALU.mult, op1=ALU.add)
                nc.sync.dma_start(out=out[bt * P:(bt + 1) * P, k * D:(k + 1) * D], in_=z[:])

        with tc.tile_pool(name="tri", bufs=1) as tri_pool:
            tri_sb = [tri_pool.tile([P, NC * APC], BF16, name="tri%d" % bt) for bt in range(NBT)]
            nc.sync.dma_start(out=b1rows[0:2 * NC, :], in_=b1.rearrange("k (g c) -> (k g) c", g=2))
            for v, vec in enumerate((b2, gamma, beta)):
                nc.sync.dma_start(out=vrows[v][0:NC, :], in_=vec)
            for i in range(NBT):
                load_w(i // 2, i % 2)
                nc.sync.dma_start(out=tri_sb[i][:], in_=tri[i * P:(i + 1) * P, :])
            if SIGMA:
                nc.vector.tensor_copy(out=b1cols[:].rearrange("p t (q r) -> p t q r", r=8),
                                      in_=b1rows[:].rearrange("p (q t r) -> p t q r", t=4, r=8))
            else:
                nc.vector.tensor_copy(out=b1cols[:], in_=b1rows[:].rearrange("p (m t) -> p t m", t=4))
            b1p = psum.tile([P, 4, P], BF16, name="b1p", tag="bank")
            for t in range(4):
                nc.tensor.transpose(b1p[:, t, :], b1cols[:, t, :], ident[:])
            nc.scalar.copy(out=b1T[:], in_=b1p[:, :, 0:2 * NC])
            for kk in range(NC // 2):
                bb = psum.tile([P, 2, D], BF16, name="bb", tag="bank")
                spread(bb[:, 0, :], 0, 2 * kk)
                spread(bb[:, 1, :], 0, 2 * kk + 1)
                nc.scalar.copy(out=b2b[:, 2 * kk * D:(2 * kk + 2) * D], in_=bb[:].rearrange("p a d -> p (a d)"))
            for j in range(HEAD_STEPS):
                fill(1)
                quant_x(4 * j - 3)
                for n in range(2 * j, min(2 * j + 2, NX)):
                    xpose_evac(tri_sb, n)

        late = {"r": ctx.enter_context(tc.tile_pool(name="r", bufs=2)),
                "gh": ctx.enter_context(tc.tile_pool(name="gh", bufs=2)),
                "ln": ctx.enter_context(tc.tile_pool(name="ln", bufs=4))}
        mm1(0, 0)

        for i in range(NC + 1):
            cur = i < NC
            prev = i >= 1
            share = [(FILL[i] + 3 - s) // 4 for s in range(4)] if cur else [0, 0, 0, 0]
            if prev:
                quant_h(i - 1, 1)
                mm2(i - 1)
            else:
                quant_x(2 * NX)
            if cur:
                relu(late, i, 0)
                mm1(i, 1)
            fill(share[0])
            if prev:
                add_bias(late, i - 1, (0, 1, 2))
                mean(i - 1, 0)
                add_bias(late, i - 1, (3,))
            if cur:
                square(late, i, 0)
            fill(share[1])
            if prev:
                mean(i - 1, 1)
                variance(late, i - 1, 0)
            if cur:
                quant_h(i, 0)
                if i + 1 < NC:
                    mm1(i + 1, 0)
                relu(late, i, 1)
            if prev:
                invert(i - 1, 0)
                centre_gain(late, i - 1, 0)
                centre_gain(late, i - 1, 1)
                variance(late, i - 1, 1)
            fill(share[2])
            if prev:
                invert(i - 1, 1)
                scale_shift_store(late, i - 1, 0)
            if cur:
                square(late, i, 1)
            fill(share[3])
            if prev:
                scale_shift_store(late, i - 1, 1)
